import numpy as np
import ml_dtypes


def mxq(x, axis, fmt="e4m3"):
    dtype, down = {"e4m3": (ml_dtypes.float8_e4m3fn, 7), "e5m2": (ml_dtypes.float8_e5m2, 14)}[fmt]
    v = np.moveaxis(np.asarray(x, np.float32).astype(ml_dtypes.bfloat16).astype(np.float64), axis, -1)
    blocks = v.reshape(v.shape[:-1] + (-1, 32))
    amax = np.abs(blocks).max(-1, keepdims=True)
    byte = np.maximum(np.where(amax > 0, np.frexp(amax)[1] - 1 + 127, 0) - down, 1)
    scale = np.exp2(byte - 127.0)
    codes = (blocks / scale).astype(np.float32).astype(dtype).astype(np.float64)
    return np.moveaxis((codes * scale).reshape(v.shape), -1, axis)


WIDE = False


def mx_kscale(k):
    if not WIDE:
        return np.ones(k)
    levels = np.array([10, -10, 5, -5, 0])
    a = np.random.permutation(np.resize(levels, k // 512 * 4)).reshape(k // 512, 4)
    idx = np.arange(k)
    return np.exp2(a[idx // 512, idx % 128 // 32])


BF16 = ml_dtypes.bfloat16


def bf(x):
    return np.asarray(x, np.float32).astype(BF16)


def f64(x):
    return np.asarray(x).astype(np.float64)


B, NC, L, H, P, G, N = 1, 8, 512, 4, 256, 1, 128
S = NC * L


def setup_inputs():
    s = mx_kscale(L)
    return {
        "cb": bf(np.random.standard_normal((B, NC, G, L, L)) * 2.0 / np.sqrt(L) * s),
        "x": bf(np.random.standard_normal((B, S, H, P))),
        "dt": bf(np.random.uniform(size=(B, H, NC, L)) / s),
        "dA_cumsum": bf(np.random.uniform(size=(B, H, NC, L))),
        "C": bf(np.random.standard_normal((B, S, G, N))),
        "prev_states": bf(np.random.standard_normal((B, NC, H, P, N)) / np.sqrt(N)),
        "D": bf(np.random.standard_normal(H)),
    }


def reference(cb, x, dt, dA_cumsum, C, prev_states, D):
    cb, x, dt, dA, C, prev_states, D = f64(cb), f64(x), f64(dt), f64(dA_cumsum), f64(C), f64(prev_states), f64(D)
    rep = H // G
    C_exp = np.repeat(C, rep, axis=2)
    cb_exp = np.repeat(cb, rep, axis=2)
    decay = np.exp(dA[:, :, :, :, None] - dA[:, :, :, None, :])
    scores = cb_exp * decay.transpose(0, 2, 1, 3, 4)
    scores = np.where(np.tril(np.ones((L, L), bool)), scores, 0.0)
    x_chunks = x.reshape(B, NC, L, H, P)
    xdt = dt.transpose(0, 2, 1, 3)[..., None] * x_chunks.transpose(0, 1, 3, 2, 4)
    out = (mxq(scores, 4, "e4m3") @ mxq(xdt, 3, "e4m3")).transpose(0, 1, 3, 2, 4)
    state_decay_out = np.exp(dA.transpose(0, 2, 3, 1))[..., None]
    C_chunks = C_exp.reshape(B, NC, L, H, N)
    out_prev = (C_chunks.transpose(0, 1, 3, 2, 4) @ prev_states.transpose(0, 1, 2, 4, 3)).transpose(0, 1, 3, 2, 4) * state_decay_out
    out = (out + out_prev).reshape(B, S, H, P)
    return out + x * D[:, None]

@@ -1,0 +1,290 @@
+from contextlib import ExitStack
+
+import concourse.mybir as mybir
+from concourse.masks import make_identity
+
+FLOPS = 2 * 32 * 512 * 512 * 256 + 2 * 32 * 512 * 256 * 128
+
+BF16 = mybir.dt.bfloat16
+F32 = mybir.dt.float32
+U32 = mybir.dt.uint32
+U8 = mybir.dt.uint8
+FP8X4 = mybir.dt.float8_e4m3fn_x4
+ACT = mybir.ActivationFunctionType
+ALU = mybir.AluOpType
+
+P = 128
+NCH = 8
+NH = 4
+L = 512
+NB = 4
+HD = 256
+UNITS = NCH * NH
+BIG = 3.0e38
+
+
+def tile_model_t_kernel(tc, cb, x, dt, dA_cumsum, C, prev_states, D, out):
+    nc = tc.nc
+
+    cb_v = cb.rearrange("b c g (i m) s -> (b c g) m i s", m=P)
+    x_v = x.rearrange("b (c j p) h d -> (b c) p j (h d)", j=NB, p=P)
+    out_v = out.rearrange("b (c i p) h d -> (b c) p i (h d)", i=NB, p=P)
+    c_v = C.rearrange("b (c i m) g n -> (b c) m i (g n)", i=NB, m=P)
+    pv_v = prev_states.rearrange("b c h (q m) n -> (b c) m (h q) n", m=P)
+    da_rows_v = dA_cumsum.rearrange("b h c (i m) -> (b h c i) m", m=P)
+    dt_rows_v = dt.rearrange("b h c (i m) -> (b h c i) m", m=P)
+
+    with ExitStack() as ctx:
+        const = ctx.enter_context(tc.tile_pool(name="const", bufs=1))
+        loads = ctx.enter_context(tc.tile_pool(name="loads", bufs=2))
+        work = ctx.enter_context(tc.tile_pool(name="work", bufs=2))
+        psum = ctx.enter_context(tc.psum_pool(name="psum", bufs=1))
+        ctx.enter_context(tc.manual_schedule())
+
+        chunk = {}
+        unit = {}
+
+        def col(c, h, i):
+            return h * (NCH * NB) + c * NB + i
+
+        def load_chunk(c):
+            bc = loads.tile([P, NH, L], BF16, name="bc", tag="bc", bufs=3)
+            nc.sync.dma_start(out=bc[:], in_=dA_cumsum[0, :, c, :].partition_broadcast(P))
+            cbt = loads.tile([P, NB, L], BF16, name="cbt", tag="cbt", bufs=2)
+            nc.sync.dma_start(out=cbt[:], in_=cb_v[c])
+            xt = loads.tile([P, NB, NH * HD], BF16, name="xt", tag="xt", bufs=3)
+            nc.sync.dma_start(out=xt[:], in_=x_v[c])
+            pv = loads.tile([P, 2 * NH, P], BF16, name="pv", tag="pv", bufs=2)
+            nc.sync.dma_start(out=pv[:], in_=pv_v[c])
+            cc = loads.tile([P, NB, P], BF16, name="cc", tag="cc", bufs=2)
+            nc.sync.dma_start(out=cc[:], in_=c_v[c])
+            chunk[c] = {"bc": bc, "cbt": cbt, "xt": xt, "pv": pv, "cc": cc}
+
+        da_rows = const.tile([P, P], BF16, name="da_rows")
+        nc.sync.dma_start(out=da_rows[:], in_=da_rows_v)
+        dt_rows = const.tile([P, P], BF16, name="dt_rows")
+        nc.sync.dma_start(out=dt_rows[:], in_=dt_rows_v)
+        d_bf = const.tile([P, NH], BF16, name="d_bf")
+        nc.sync.dma_start(out=d_bf[:], in_=D.partition_broadcast(P))
+        load_chunk(0)
+        load_chunk(1)
+
+        ident = const.tile([P, P], BF16, name="ident")
+        make_identity(nc, ident[:])
+        maskf = const.tile([P, P], F32, name="maskf")
+        nc.gpsimd.memset(maskf[:], 1.0)
+        nc.gpsimd.affine_select(
+            out=maskf[:],
+            in_=maskf[:],
+            compare_op=ALU.is_ge,
+            fill=0.0,
+            base=0,
+            pattern=[[-1, P]],
+            channel_multiplier=1,
+        )
+        maskb = const.tile([P, P], BF16, name="maskb")
+        nc.vector.tensor_copy(out=maskb[:], in_=maskf[:])
+
+        wgs = []
+        for k in range(2):
+            wg = const.tile([P, L * NB], BF16, name="wg%d" % k, align_bytes=64)
+            nc.vector.memset(wg[:], 0.0)
+            wgs.append(wg)
+
+        d_col = const.tile([P, NH], F32, name="d_col")
+        nc.vector.tensor_copy(out=d_col[:], in_=d_bf[:])
+
+        da_t = psum.tile([P, P], BF16, name="da_t", tag="tp", bufs=2)
+        nc.tensor.transpose(out=da_t[:], in_=da_rows[:], identity=ident[:])
+        e_a = const.tile([P, P], F32, name="e_a")
+        nc.scalar.activation(out=e_a[:], in_=da_t[:], func=ACT.Exp)
+        neg_da = const.tile([P, P], F32, name="neg_da")
+        nc.scalar.activation(out=neg_da[:], in_=da_t[:], func=ACT.Copy, scale=-1.0)
+        dt_t = psum.tile([P, P], BF16, name="dt_t", tag="tp", bufs=2)
+        nc.tensor.transpose(out=dt_t[:], in_=dt_rows[:], identity=ident[:])
+        dt_col = const.tile([P, P], F32, name="dt_col")
+        nc.scalar.copy(out=dt_col[:], in_=dt_t[:])
+
+        def mask_chunk(c):
+            cbt = chunk[c]["cbt"]
+            for i in range(NB):
+                blk = cbt[:, i, i * P : (i + 1) * P]
+                nc.gpsimd.tensor_tensor(out=blk, in0=blk, in1=maskb[:], op=ALU.mult)
+
+        def prep_chunk(c):
+            cc_t = psum.tile([P, NB, P], BF16, name="cc_t", tag="tp", bufs=2)
+            for i in range(NB):
+                nc.tensor.transpose(out=cc_t[:, i, :], in_=chunk[c]["cc"][:, i, :], identity=ident[:])
+            ct = work.tile([P, NB, P], BF16, name="ct", tag="ct", bufs=2)
+            nc.vector.tensor_copy(out=ct[:], in_=cc_t[:])
+            pv_t = psum.tile([P, 2 * NH, P], BF16, name="pv_t", tag="tp", bufs=2)
+            for q in range(2 * NH):
+                nc.tensor.transpose(out=pv_t[:, q, :], in_=chunk[c]["pv"][:, q, :], identity=ident[:])
+            pt = work.tile([P, 2 * NH, P], BF16, name="pt", tag="pt", bufs=2)
+            nc.scalar.copy(out=pt[:], in_=pv_t[:])
+            chunk[c]["ct"] = ct
+            chunk[c]["pt"] = pt
+
+        def cbt_chunk(c):
+            cbt = chunk[c]["cbt"]
+            ta = psum.tile([P, 6 * P], BF16, name="cbta", tag="cbta", bufs=1)
+            tb = psum.tile([P, 4 * P], BF16, name="cbtb", tag="cbtb", bufs=1)
+            views = []
+            off = 0
+            for i in range(NB):
+                if i < 3:
+                    v = ta[:, off : off + (i + 1) * P]
+                    off += (i + 1) * P
+                else:
+                    v = tb[:]
+                v = v.rearrange("p (j l) -> p j l", l=P)
+                for j in range(i + 1):
+                    nc.tensor.transpose(out=v[:, j, :], in_=cbt[:, i, j * P : (j + 1) * P], identity=ident[:])
+                views.append(v)
+            chunk[c]["cbT"] = views
+
+        def stage_s(u):
+            c, h = divmod(u, NH)
+            dec = work.tile([P, NB, L], F32, name="dec", tag="dec", bufs=2)
+            for j in range(NB):
+                k = col(c, h, j)
+                nc.scalar.activation(
+                    out=dec[:, j, j * P :],
+                    in_=chunk[c]["bc"][:, h, j * P :],
+                    func=ACT.Exp,
+                    bias=neg_da[:, k : k + 1],
+                    scale=1.0,
+                )
+            up = work.tile([P, NB, HD], BF16, name="up", tag="up", bufs=2)
+            for j in range(NB):
+                k = col(c, h, j)
+                nc.scalar.activation(
+                    out=up[:, j, :],
+                    in_=chunk[c]["xt"][:, j, h * HD : (h + 1) * HD],
+                    func=ACT.Copy,
+                    scale=dt_col[:, k : k + 1],
+                )
+            unit[u] = {"dec": dec, "up": up}
+
+        def stage_z(u):
+            c, h = divmod(u, NH)
+            tz = work.tile([P, NB, HD], F32, name="tz", tag="tz", bufs=3)
+            for a in range(2):
+                z = psum.tile([P, 2, HD], F32, name="z", tag="z", bufs=2)
+                for b in range(2):
+                    i = 2 * a + b
+                    nc.tensor.matmul(
+                        out=z[:, b, :],
+                        lhsT=chunk[c]["ct"][:, i, :],
+                        rhs=chunk[c]["pt"][:, 2 * h : 2 * h + 2, :].rearrange("p q m -> p (q m)"),
+                        start=True,
+                        stop=True,
+                    )
+                for b in range(2):
+                    i = 2 * a + b
+                    k = col(c, h, i)
+                    nc.scalar.activation(out=tz[:, i, :], in_=z[:, b, :], func=ACT.Copy, scale=e_a[:, k : k + 1])
+            unit[u]["tz"] = tz
+
+        def stage_w(u):
+            c, h = divmod(u, NH)
+            wg3 = wgs[u % 2][:].rearrange("p (l j) -> p l j", j=NB)
+            dec = unit[u]["dec"]
+            for i in range(NB):
+                nc.vector.scalar_tensor_tensor(
+                    out=wg3[:, i * P : (i + 1) * P, 0 : i + 1],
+                    in0=dec[:, 0 : i + 1, i * P : (i + 1) * P].rearrange("p j l -> p l j"),
+                    scalar=BIG,
+                    in1=chunk[c]["cbT"][i].rearrange("p j l -> p l j"),
+                    op0=ALU.min,
+                    op1=ALU.mult,
+                )
+            ug = work.tile([P, HD, NB], BF16, name="ug", tag="ug", bufs=2, align_bytes=64)
+            nc.vector.tensor_copy(
+                out=ug[:].rearrange("p (c i) t -> p c t i", i=4),
+                in_=unit[u]["up"][:].rearrange("p t (c i) -> p c t i", i=4),
+            )
+            unit[u]["ug"] = ug
+
+        def quant_w(u):
+            wq = work.tile([P, L], U32, name="wq", tag="wq", bufs=2, align_bytes=64)
+            ws = work.tile([P, L], U8, name="ws", tag="ws", bufs=2, align_bytes=64)
+            nc.vector.quantize_mx(out=wq[:].bitcast(FP8X4), scales=ws[:], in_=wgs[u % 2][:])
+            unit[u]["wq"] = wq
+            unit[u]["ws"] = ws
+
+        def quant_u(u):
+            uq = work.tile([P, HD], U32, name="uq", tag="uq", bufs=2, align_bytes=64)
+            us = work.tile([P, HD], U8, name="us", tag="us", bufs=2, align_bytes=64)
+            nc.vector.quantize_mx(
+                out=uq[:].bitcast(FP8X4), scales=us[:], in_=unit[u]["ug"][:].rearrange("p c t -> p (c t)")
+            )
+            unit[u]["uq"] = uq
+            unit[u]["us"] = us
+
+        def stage_m(u):
+            ys = []
+            for a in range(2):
+                y = psum.tile([P, 2, HD], F32, name="y", tag="y", bufs=2)
+                for b in range(2):
+                    i = 2 * a + b
+                    nc.tensor.matmul_mx(
+                        out=y[:, b, :],
+                        lhsT=unit[u]["wq"][:, i * P : (i + 1) * P].bitcast(FP8X4),
+                        lhsT_scale=unit[u]["ws"][:, i * P : (i + 1) * P],
+                        rhs=unit[u]["uq"][:].bitcast(FP8X4),
+                        rhs_scale=unit[u]["us"][:],
+                        start=True,
+                        stop=True,
+                    )
+                ys.append(y)
+            unit[u]["y"] = ys
+
+        def stage_e(u, a):
+            c, h = divmod(u, NH)
+            if a == 0:
+                unit[u]["o"] = work.tile([P, NB, HD], F32, name="o", tag="o", bufs=3)
+            nc.vector.scalar_tensor_tensor(
+                out=unit[u]["o"][:, 2 * a : 2 * a + 2, :],
+                in0=chunk[c]["xt"][:, 2 * a : 2 * a + 2, h * HD : (h + 1) * HD],
+                scalar=d_col[:, h : h + 1],
+                in1=unit[u]["y"][a][:],
+                op0=ALU.mult,
+                op1=ALU.add,
+            )
+
+        def stage_g(u):
+            c, h = divmod(u, NH)
+            o = unit[u]["o"]
+            nc.gpsimd.tensor_tensor(out=o[:], in0=o[:], in1=unit[u]["tz"][:], op=ALU.add)
+            nc.sync.dma_start(out=out_v[c][:, :, h * HD : (h + 1) * HD], in_=o[:])
+
+        mask_chunk(0)
+        cbt_chunk(0)
+        prep_chunk(0)
+        stage_s(0)
+        stage_z(0)
+        for u in range(UNITS):
+            c, h = divmod(u, NH)
+            if u + 1 < UNITS:
+                stage_s(u + 1)
+                stage_z(u + 1)
+            if h == 1 and c + 1 < NCH:
+                mask_chunk(c + 1)
+                prep_chunk(c + 1)
+            stage_w(u)
+            if h == 3 and c + 1 < NCH:
+                cbt_chunk(c + 1)
+            quant_w(u)
+            if u >= 1:
+                stage_e(u - 1, 0)
+            quant_u(u)
+            if u >= 1:
+                stage_e(u - 1, 1)
+                stage_g(u - 1)
+            stage_m(u)
+            if h == 0 and c + 2 < NCH:
+                load_chunk(c + 2)
+        stage_e(UNITS - 1, 0)
+        stage_e(UNITS - 1, 1)
+        stage_g(UNITS - 1)

@@ -21,6 +21,7 @@ NB = 4
 HD = 256
 UNITS = NCH * NH
 BIG = 3.0e38
+NDIRECT = 1
 
 
 def tile_model_t_kernel(tc, cb, x, dt, dA_cumsum, C, prev_states, D, out):
@@ -109,19 +110,23 @@ def tile_model_t_kernel(tc, cb, x, dt, dA_cumsum, C, prev_states, D, out):
             cbt = chunk[c]["cbt"]
             for i in range(NB):
                 blk = cbt[:, i, i * P : (i + 1) * P]
-                nc.gpsimd.tensor_tensor(out=blk, in0=blk, in1=maskb[:], op=ALU.mult)
+                nc.vector.tensor_tensor(out=blk, in0=blk, in1=maskb[:], op=ALU.mult)
 
-        def prep_chunk(c):
+        def prep_pe(c):
             cc_t = psum.tile([P, NB, P], BF16, name="cc_t", tag="tp", bufs=2)
             for i in range(NB):
                 nc.tensor.transpose(out=cc_t[:, i, :], in_=chunk[c]["cc"][:, i, :], identity=ident[:])
-            ct = work.tile([P, NB, P], BF16, name="ct", tag="ct", bufs=2)
-            nc.vector.tensor_copy(out=ct[:], in_=cc_t[:])
             pv_t = psum.tile([P, 2 * NH, P], BF16, name="pv_t", tag="tp", bufs=2)
             for q in range(2 * NH):
                 nc.tensor.transpose(out=pv_t[:, q, :], in_=chunk[c]["pv"][:, q, :], identity=ident[:])
+            chunk[c]["cc_t"] = cc_t
+            chunk[c]["pv_t"] = pv_t
+
+        def prep_copy(c):
+            ct = work.tile([P, NB, P], BF16, name="ct", tag="ct", bufs=2)
+            nc.vector.tensor_copy(out=ct[:], in_=chunk[c]["cc_t"][:])
             pt = work.tile([P, 2 * NH, P], BF16, name="pt", tag="pt", bufs=2)
-            nc.scalar.copy(out=pt[:], in_=pv_t[:])
+            nc.scalar.copy(out=pt[:], in_=chunk[c]["pv_t"][:])
             chunk[c]["ct"] = ct
             chunk[c]["pt"] = pt
 
@@ -145,7 +150,7 @@ def tile_model_t_kernel(tc, cb, x, dt, dA_cumsum, C, prev_states, D, out):
 
         def stage_s(u):
             c, h = divmod(u, NH)
-            dec = work.tile([P, NB, L], F32, name="dec", tag="dec", bufs=2)
+            dec = work.tile([P, NB, L], F32, name="dec", tag="dec", bufs=3)
             for j in range(NB):
                 k = col(c, h, j)
                 nc.scalar.activation(
@@ -155,7 +160,7 @@ def tile_model_t_kernel(tc, cb, x, dt, dA_cumsum, C, prev_states, D, out):
                     bias=neg_da[:, k : k + 1],
                     scale=1.0,
                 )
-            up = work.tile([P, NB, HD], BF16, name="up", tag="up", bufs=2)
+            up = work.tile([P, NB, HD], BF16, name="up", tag="up", bufs=3)
             for j in range(NB):
                 k = col(c, h, j)
                 nc.scalar.activation(
@@ -168,7 +173,8 @@ def tile_model_t_kernel(tc, cb, x, dt, dA_cumsum, C, prev_states, D, out):
 
         def stage_z(u):
             c, h = divmod(u, NH)
-            tz = work.tile([P, NB, HD], F32, name="tz", tag="tz", bufs=3)
+            tz = work.tile([P, NB - NDIRECT, HD], F32, name="tz", tag="tz", bufs=3)
+            zs = []
             for a in range(2):
                 z = psum.tile([P, 2, HD], F32, name="z", tag="z", bufs=2)
                 for b in range(2):
@@ -183,8 +189,11 @@ def tile_model_t_kernel(tc, cb, x, dt, dA_cumsum, C, prev_states, D, out):
                 for b in range(2):
                     i = 2 * a + b
                     k = col(c, h, i)
-                    nc.scalar.activation(out=tz[:, i, :], in_=z[:, b, :], func=ACT.Copy, scale=e_a[:, k : k + 1])
+                    if i < NB - NDIRECT:
+                        nc.scalar.activation(out=tz[:, i, :], in_=z[:, b, :], func=ACT.Copy, scale=e_a[:, k : k + 1])
+                zs.append(z)
             unit[u]["tz"] = tz
+            unit[u]["z"] = zs
 
         def stage_w(u):
             c, h = divmod(u, NH)
@@ -199,6 +208,8 @@ def tile_model_t_kernel(tc, cb, x, dt, dA_cumsum, C, prev_states, D, out):
                     op0=ALU.min,
                     op1=ALU.mult,
                 )
+
+        def regroup_u(u):
             ug = work.tile([P, HD, NB], BF16, name="ug", tag="ug", bufs=2, align_bytes=64)
             nc.vector.tensor_copy(
                 out=ug[:].rearrange("p (c i) t -> p c t i", i=4),
@@ -240,51 +251,61 @@ def tile_model_t_kernel(tc, cb, x, dt, dA_cumsum, C, prev_states, D, out):
                 ys.append(y)
             unit[u]["y"] = ys
 
-        def stage_e(u, a):
+        def stage_e(u):
             c, h = divmod(u, NH)
-            if a == 0:
-                unit[u]["o"] = work.tile([P, NB, HD], F32, name="o", tag="o", bufs=3)
-            nc.vector.scalar_tensor_tensor(
-                out=unit[u]["o"][:, 2 * a : 2 * a + 2, :],
-                in0=chunk[c]["xt"][:, 2 * a : 2 * a + 2, h * HD : (h + 1) * HD],
-                scalar=d_col[:, h : h + 1],
-                in1=unit[u]["y"][a][:],
-                op0=ALU.mult,
-                op1=ALU.add,
-            )
-
-        def stage_g(u):
-            c, h = divmod(u, NH)
-            o = unit[u]["o"]
-            nc.gpsimd.tensor_tensor(out=o[:], in0=o[:], in1=unit[u]["tz"][:], op=ALU.add)
+            o = work.tile([P, NB, HD], F32, name="o", tag="o", bufs=3)
+            tz = unit[u]["tz"]
+            for a in (1, 0):
+                nc.vector.scalar_tensor_tensor(
+                    out=o[:, 2 * a : 2 * a + 2, :],
+                    in0=chunk[c]["xt"][:, 2 * a : 2 * a + 2, h * HD : (h + 1) * HD],
+                    scalar=d_col[:, h : h + 1],
+                    in1=unit[u]["y"][a][:],
+                    op0=ALU.mult,
+                    op1=ALU.add,
+                )
+                lo = 2 * a
+                hi = min(2 * a + 2, NB - NDIRECT)
+                if hi > lo:
+                    nc.gpsimd.tensor_tensor(out=o[:, lo:hi, :], in0=o[:, lo:hi, :], in1=tz[:, lo:hi, :], op=ALU.add)
+            for i in range(NB - NDIRECT, NB):
+                k = col(c, h, i)
+                nc.vector.scalar_tensor_tensor(
+                    out=o[:, i, :],
+                    in0=unit[u]["z"][i // 2][:, i % 2, :],
+                    scalar=e_a[:, k : k + 1],
+                    in1=o[:, i, :],
+                    op0=ALU.mult,
+                    op1=ALU.add,
+                )
             nc.sync.dma_start(out=out_v[c][:, :, h * HD : (h + 1) * HD], in_=o[:])
 
         mask_chunk(0)
         cbt_chunk(0)
-        prep_chunk(0)
+        prep_pe(0)
+        prep_copy(0)
         stage_s(0)
-        stage_z(0)
-        for u in range(UNITS):
-            c, h = divmod(u, NH)
-            if u + 1 < UNITS:
-                stage_s(u + 1)
-                stage_z(u + 1)
-            if h == 1 and c + 1 < NCH:
-                mask_chunk(c + 1)
-                prep_chunk(c + 1)
-            stage_w(u)
-            if h == 3 and c + 1 < NCH:
-                cbt_chunk(c + 1)
-            quant_w(u)
-            if u >= 1:
-                stage_e(u - 1, 0)
-            quant_u(u)
-            if u >= 1:
-                stage_e(u - 1, 1)
-                stage_g(u - 1)
-            stage_m(u)
-            if h == 0 and c + 2 < NCH:
-                load_chunk(c + 2)
-        stage_e(UNITS - 1, 0)
-        stage_e(UNITS - 1, 1)
-        stage_g(UNITS - 1)
+        for k in range(UNITS + 2):
+            c, h = divmod(k, NH)
+            if k + 1 < UNITS:
+                stage_s(k + 1)
+            if k >= 2:
+                stage_e(k - 2)
+            if 1 <= k <= UNITS:
+                stage_m(k - 1)
+                stage_z(k - 1)
+            if k < UNITS:
+                if h == 2 and c + 1 < NCH:
+                    prep_pe(c + 1)
+                stage_w(k)
+                if h == 2 and c + 1 < NCH:
+                    prep_copy(c + 1)
+                if h == 3 and c + 1 < NCH:
+                    cbt_chunk(c + 1)
+                if h == 1 and c + 1 < NCH:
+                    mask_chunk(c + 1)
+                regroup_u(k)
+                quant_w(k)
+                quant_u(k)
+                if h == 1 and c + 2 < NCH:
+                    load_chunk(c + 2)

@@ -22,6 +22,7 @@ HD = 256
 UNITS = NCH * NH
 BIG = 3.0e38
 NDIRECT = 1
+CB_PITCH = 640
 
 
 def tile_model_t_kernel(tc, cb, x, dt, dA_cumsum, C, prev_states, D, out):
@@ -48,25 +49,29 @@ def tile_model_t_kernel(tc, cb, x, dt, dA_cumsum, C, prev_states, D, out):
         def col(c, h, i):
             return h * (NCH * NB) + c * NB + i
 
+        def ndirect(u):
+            return NB if u == UNITS - 1 else NDIRECT
+
         def load_chunk(c):
+            cbf = loads.tile([P, NB * (CB_PITCH + P)], BF16, name="cbf", tag="cbf", bufs=2)
+            cbt = cbf[:, 0 : NB * CB_PITCH].rearrange("p (i w) -> p i w", w=CB_PITCH)[:, :, 0:L]
+            nc.sync.dma_start(out=cbt, in_=cb_v[c])
             bc = loads.tile([P, NH, L], BF16, name="bc", tag="bc", bufs=3)
             nc.sync.dma_start(out=bc[:], in_=dA_cumsum[0, :, c, :].partition_broadcast(P))
-            cbt = loads.tile([P, NB, L], BF16, name="cbt", tag="cbt", bufs=2)
-            nc.sync.dma_start(out=cbt[:], in_=cb_v[c])
             xt = loads.tile([P, NB, NH * HD], BF16, name="xt", tag="xt", bufs=3)
             nc.sync.dma_start(out=xt[:], in_=x_v[c])
             pv = loads.tile([P, 2 * NH, P], BF16, name="pv", tag="pv", bufs=2)
             nc.sync.dma_start(out=pv[:], in_=pv_v[c])
             cc = loads.tile([P, NB, P], BF16, name="cc", tag="cc", bufs=2)
             nc.sync.dma_start(out=cc[:], in_=c_v[c])
-            chunk[c] = {"bc": bc, "cbt": cbt, "xt": xt, "pv": pv, "cc": cc}
+            chunk[c] = {"bc": bc, "cbf": cbf, "cbt": cbt, "xt": xt, "pv": pv, "cc": cc}
 
         da_rows = const.tile([P, P], BF16, name="da_rows")
-        nc.sync.dma_start(out=da_rows[:], in_=da_rows_v)
+        nc.scalar.dma_start(out=da_rows[:], in_=da_rows_v)
         dt_rows = const.tile([P, P], BF16, name="dt_rows")
-        nc.sync.dma_start(out=dt_rows[:], in_=dt_rows_v)
+        nc.scalar.dma_start(out=dt_rows[:], in_=dt_rows_v)
         d_bf = const.tile([P, NH], BF16, name="d_bf")
-        nc.sync.dma_start(out=d_bf[:], in_=D.partition_broadcast(P))
+        nc.scalar.dma_start(out=d_bf[:], in_=D.partition_broadcast(P))
         load_chunk(0)
         load_chunk(1)
 
@@ -107,10 +112,10 @@ def tile_model_t_kernel(tc, cb, x, dt, dA_cumsum, C, prev_states, D, out):
         nc.scalar.copy(out=dt_col[:], in_=dt_t[:])
 
         def mask_chunk(c):
-            cbt = chunk[c]["cbt"]
-            for i in range(NB):
-                blk = cbt[:, i, i * P : (i + 1) * P]
-                nc.vector.tensor_tensor(out=blk, in0=blk, in1=maskb[:], op=ALU.mult)
+            diag = chunk[c]["cbf"][:].rearrange("p (i w) -> p i w", w=CB_PITCH + P)[:, :, 0:P]
+            nc.vector.tensor_tensor(
+                out=diag, in0=diag, in1=maskb[:].unsqueeze(1).to_broadcast([P, NB, P]), op=ALU.mult
+            )
 
         def prep_pe(c):
             cc_t = psum.tile([P, NB, P], BF16, name="cc_t", tag="tp", bufs=2)
@@ -170,10 +175,15 @@ def tile_model_t_kernel(tc, cb, x, dt, dA_cumsum, C, prev_states, D, out):
                     scale=dt_col[:, k : k + 1],
                 )
             unit[u] = {"dec": dec, "up": up}
+            if h != 0:
+                regroup_u(u, nc.scalar.copy)
 
         def stage_z(u):
             c, h = divmod(u, NH)
-            tz = work.tile([P, NB - NDIRECT, HD], F32, name="tz", tag="tz", bufs=3)
+            nd = ndirect(u)
+            tz = None
+            if nd < NB:
+                tz = work.tile([P, NB - nd, HD], F32, name="tz", tag="tz", bufs=3)
             zs = []
             for a in range(2):
                 z = psum.tile([P, 2, HD], F32, name="z", tag="z", bufs=2)
@@ -189,7 +199,7 @@ def tile_model_t_kernel(tc, cb, x, dt, dA_cumsum, C, prev_states, D, out):
                 for b in range(2):
                     i = 2 * a + b
                     k = col(c, h, i)
-                    if i < NB - NDIRECT:
+                    if i < NB - nd:
                         nc.scalar.activation(out=tz[:, i, :], in_=z[:, b, :], func=ACT.Copy, scale=e_a[:, k : k + 1])
                 zs.append(z)
             unit[u]["tz"] = tz
@@ -209,9 +219,9 @@ def tile_model_t_kernel(tc, cb, x, dt, dA_cumsum, C, prev_states, D, out):
                     op1=ALU.mult,
                 )
 
-        def regroup_u(u):
-            ug = work.tile([P, HD, NB], BF16, name="ug", tag="ug", bufs=2, align_bytes=64)
-            nc.vector.tensor_copy(
+        def regroup_u(u, copier):
+            ug = work.tile([P, HD, NB], BF16, name="ug", tag="ug", bufs=3, align_bytes=64)
+            copier(
                 out=ug[:].rearrange("p (c i) t -> p c t i", i=4),
                 in_=unit[u]["up"][:].rearrange("p t (c i) -> p c t i", i=4),
             )
@@ -255,6 +265,7 @@ def tile_model_t_kernel(tc, cb, x, dt, dA_cumsum, C, prev_states, D, out):
             c, h = divmod(u, NH)
             o = work.tile([P, NB, HD], F32, name="o", tag="o", bufs=3)
             tz = unit[u]["tz"]
+            nd = ndirect(u)
             for a in (1, 0):
                 nc.vector.scalar_tensor_tensor(
                     out=o[:, 2 * a : 2 * a + 2, :],
@@ -265,10 +276,10 @@ def tile_model_t_kernel(tc, cb, x, dt, dA_cumsum, C, prev_states, D, out):
                     op1=ALU.add,
                 )
                 lo = 2 * a
-                hi = min(2 * a + 2, NB - NDIRECT)
+                hi = min(2 * a + 2, NB - nd)
                 if hi > lo:
                     nc.gpsimd.tensor_tensor(out=o[:, lo:hi, :], in0=o[:, lo:hi, :], in1=tz[:, lo:hi, :], op=ALU.add)
-            for i in range(NB - NDIRECT, NB):
+            for i in reversed(range(NB - nd, NB)):
                 k = col(c, h, i)
                 nc.vector.scalar_tensor_tensor(
                     out=o[:, i, :],
@@ -278,7 +289,12 @@ def tile_model_t_kernel(tc, cb, x, dt, dA_cumsum, C, prev_states, D, out):
                     op0=ALU.mult,
                     op1=ALU.add,
                 )
-            nc.sync.dma_start(out=out_v[c][:, :, h * HD : (h + 1) * HD], in_=o[:])
+                if nd == NB and i == 2:
+                    nc.sync.dma_start(out=out_v[c][:, 2:NB, h * HD : (h + 1) * HD], in_=o[:, 2:NB, :])
+            if nd == NB:
+                nc.sync.dma_start(out=out_v[c][:, 0:2, h * HD : (h + 1) * HD], in_=o[:, 0:2, :])
+            else:
+                nc.sync.dma_start(out=out_v[c][:, :, h * HD : (h + 1) * HD], in_=o[:])
 
         mask_chunk(0)
         cbt_chunk(0)
@@ -304,8 +320,12 @@ def tile_model_t_kernel(tc, cb, x, dt, dA_cumsum, C, prev_states, D, out):
                     cbt_chunk(c + 1)
                 if h == 1 and c + 1 < NCH:
                     mask_chunk(c + 1)
-                regroup_u(k)
-                quant_w(k)
-                quant_u(k)
+                if h == 0:
+                    regroup_u(k, nc.vector.tensor_copy)
+                    quant_w(k)
+                    quant_u(k)
+                else:
+                    quant_u(k)
+                    quant_w(k)
                 if h == 1 and c + 2 < NCH:
                     load_chunk(c + 2)

@@ -21,7 +21,8 @@ NB = 4
 HD = 256
 UNITS = NCH * NH
 BIG = 3.0e38
-NDIRECT = 1
+NDIRECT = 0
+S_PLANES = 1
 CB_PITCH = 640
 
 
@@ -129,7 +130,7 @@ def tile_model_t_kernel(tc, cb, x, dt, dA_cumsum, C, prev_states, D, out):
 
         def prep_copy(c):
             ct = work.tile([P, NB, P], BF16, name="ct", tag="ct", bufs=2)
-            nc.vector.tensor_copy(out=ct[:], in_=chunk[c]["cc_t"][:])
+            nc.scalar.copy(out=ct[:], in_=chunk[c]["cc_t"][:])
             pt = work.tile([P, 2 * NH, P], BF16, name="pt", tag="pt", bufs=2)
             nc.scalar.copy(out=pt[:], in_=chunk[c]["pv_t"][:])
             chunk[c]["ct"] = ct
@@ -165,25 +166,33 @@ def tile_model_t_kernel(tc, cb, x, dt, dA_cumsum, C, prev_states, D, out):
                     bias=neg_da[:, k : k + 1],
                     scale=1.0,
                 )
-            up = work.tile([P, NB, HD], BF16, name="up", tag="up", bufs=3)
-            for j in range(NB):
+            for j in range(S_PLANES):
                 k = col(c, h, j)
                 nc.scalar.activation(
-                    out=up[:, j, :],
+                    out=unit[u]["up"][:, j, :],
                     in_=chunk[c]["xt"][:, j, h * HD : (h + 1) * HD],
                     func=ACT.Copy,
                     scale=dt_col[:, k : k + 1],
                 )
-            unit[u] = {"dec": dec, "up": up}
-            if h != 0:
-                regroup_u(u, nc.scalar.copy)
+            unit[u]["dec"] = dec
+            regroup_u(u, nc.scalar.copy)
+
+        def planes_v(u):
+            c, h = divmod(u, NH)
+            up = work.tile([P, NB, HD], BF16, name="up", tag="up", bufs=3)
+            for j in range(S_PLANES, NB):
+                k = col(c, h, j)
+                nc.vector.tensor_scalar_mul(
+                    out=up[:, j, :], in0=chunk[c]["xt"][:, j, h * HD : (h + 1) * HD], scalar1=dt_col[:, k : k + 1]
+                )
+            unit[u] = {"up": up}
 
         def stage_z(u):
             c, h = divmod(u, NH)
             nd = ndirect(u)
             tz = None
             if nd < NB:
-                tz = work.tile([P, NB - nd, HD], F32, name="tz", tag="tz", bufs=3)
+                tz = work.tile([P, NB - nd, HD], F32, name="tz", tag="tz", bufs=4)
             zs = []
             for a in range(2):
                 z = psum.tile([P, 2, HD], F32, name="z", tag="z", bufs=2)
@@ -298,18 +307,22 @@ def tile_model_t_kernel(tc, cb, x, dt, dA_cumsum, C, prev_states, D, out):
 
         mask_chunk(0)
         cbt_chunk(0)
-        prep_pe(0)
-        prep_copy(0)
+        planes_v(0)
+        planes_v(1)
         stage_s(0)
         for k in range(UNITS + 2):
             c, h = divmod(k, NH)
             if k + 1 < UNITS:
                 stage_s(k + 1)
+            if k == 0:
+                prep_pe(0)
+                prep_copy(0)
+            if k < UNITS:
+                stage_z(k)
             if k >= 2:
                 stage_e(k - 2)
             if 1 <= k <= UNITS:
                 stage_m(k - 1)
-                stage_z(k - 1)
             if k < UNITS:
                 if h == 2 and c + 1 < NCH:
                     prep_pe(c + 1)
@@ -320,12 +333,9 @@ def tile_model_t_kernel(tc, cb, x, dt, dA_cumsum, C, prev_states, D, out):
                     cbt_chunk(c + 1)
                 if h == 1 and c + 1 < NCH:
                     mask_chunk(c + 1)
-                if h == 0:
-                    regroup_u(k, nc.vector.tensor_copy)
-                    quant_w(k)
-                    quant_u(k)
-                else:
-                    quant_u(k)
-                    quant_w(k)
+                if k + 2 < UNITS:
+                    planes_v(k + 2)
+                quant_u(k)
+                quant_w(k)
                 if h == 1 and c + 2 < NCH:
                     load_chunk(c + 2)

@@ -42,7 +42,6 @@ def tile_model_t_kernel(tc, cb, x, dt, dA_cumsum, C, prev_states, D, out):
         loads = ctx.enter_context(tc.tile_pool(name="loads", bufs=2))
         work = ctx.enter_context(tc.tile_pool(name="work", bufs=2))
         psum = ctx.enter_context(tc.psum_pool(name="psum", bufs=1))
-        ctx.enter_context(tc.manual_schedule())
 
         chunk = {}
         unit = {}

@@ -22,7 +22,6 @@ HD = 256
 UNITS = NCH * NH
 BIG = 3.0e38
 NDIRECT = 0
-S_PLANES = 1
 CB_PITCH = 640
 
 
@@ -42,12 +41,16 @@ def tile_model_t_kernel(tc, cb, x, dt, dA_cumsum, C, prev_states, D, out):
         loads = ctx.enter_context(tc.tile_pool(name="loads", bufs=2))
         work = ctx.enter_context(tc.tile_pool(name="work", bufs=2))
         psum = ctx.enter_context(tc.psum_pool(name="psum", bufs=1))
+        ctx.enter_context(tc.manual_schedule())
 
         chunk = {}
         unit = {}
 
         def col(c, h, i):
             return h * (NCH * NB) + c * NB + i
+
+        def s_planes(u):
+            return u % 2
 
         def ndirect(u):
             return NB if u == UNITS - 1 else NDIRECT
@@ -97,6 +100,14 @@ def tile_model_t_kernel(tc, cb, x, dt, dA_cumsum, C, prev_states, D, out):
             nc.vector.memset(wg[:], 0.0)
             wgs.append(wg)
 
+        decs = []
+        for k in range(3):
+            dec_k = const.tile([P, NB, L], F32, name="dec%d" % k)
+            nc.vector.memset(dec_k[:, 1, 0:P], 0.0)
+            decs.append(dec_k)
+        zeros = const.tile([P, P], BF16, name="zeros")
+        nc.vector.memset(zeros[:], 0.0)
+
         d_col = const.tile([P, NH], F32, name="d_col")
         nc.vector.tensor_copy(out=d_col[:], in_=d_bf[:])
 
@@ -137,25 +148,24 @@ def tile_model_t_kernel(tc, cb, x, dt, dA_cumsum, C, prev_states, D, out):
 
         def cbt_chunk(c):
             cbt = chunk[c]["cbt"]
-            ta = psum.tile([P, 6 * P], BF16, name="cbta", tag="cbta", bufs=1)
+            ta = psum.tile([P, 7 * P], BF16, name="cbta", tag="cbta", bufs=1)
             tb = psum.tile([P, 4 * P], BF16, name="cbtb", tag="cbtb", bufs=1)
-            views = []
-            off = 0
-            for i in range(NB):
-                if i < 3:
-                    v = ta[:, off : off + (i + 1) * P]
-                    off += (i + 1) * P
-                else:
-                    v = tb[:]
-                v = v.rearrange("p (j l) -> p j l", l=P)
-                for j in range(i + 1):
-                    nc.tensor.transpose(out=v[:, j, :], in_=cbt[:, i, j * P : (j + 1) * P], identity=ident[:])
-                views.append(v)
-            chunk[c]["cbT"] = views
+            v01 = ta[:, 0 : 4 * P].rearrange("p (j l) -> p j l", j=2)
+            v2 = ta[:, 4 * P : 7 * P].rearrange("p (j l) -> p j l", j=3)
+            v3 = tb[:].rearrange("p (j l) -> p j l", j=4)
+            nc.tensor.transpose(out=v01[:, 0, 0:P], in_=cbt[:, 0, 0:P], identity=ident[:])
+            nc.tensor.transpose(out=v01[:, 1, 0:P], in_=zeros[:], identity=ident[:])
+            for j in range(2):
+                nc.tensor.transpose(out=v01[:, j, P : 2 * P], in_=cbt[:, 1, j * P : (j + 1) * P], identity=ident[:])
+            for j in range(3):
+                nc.tensor.transpose(out=v2[:, j, :], in_=cbt[:, 2, j * P : (j + 1) * P], identity=ident[:])
+            for j in range(4):
+                nc.tensor.transpose(out=v3[:, j, :], in_=cbt[:, 3, j * P : (j + 1) * P], identity=ident[:])
+            chunk[c]["cbT"] = [(0, 2 * P, 2, v01), (2 * P, P, 3, v2), (3 * P, P, 4, v3)]
 
         def stage_s(u):
             c, h = divmod(u, NH)
-            dec = work.tile([P, NB, L], F32, name="dec", tag="dec", bufs=3)
+            dec = decs[u % 3]
             for j in range(NB):
                 k = col(c, h, j)
                 nc.scalar.activation(
@@ -165,7 +175,7 @@ def tile_model_t_kernel(tc, cb, x, dt, dA_cumsum, C, prev_states, D, out):
                     bias=neg_da[:, k : k + 1],
                     scale=1.0,
                 )
-            for j in range(S_PLANES):
+            for j in range(s_planes(u)):
                 k = col(c, h, j)
                 nc.scalar.activation(
                     out=unit[u]["up"][:, j, :],
@@ -179,7 +189,7 @@ def tile_model_t_kernel(tc, cb, x, dt, dA_cumsum, C, prev_states, D, out):
         def planes_v(u):
             c, h = divmod(u, NH)
             up = work.tile([P, NB, HD], BF16, name="up", tag="up", bufs=3)
-            for j in range(S_PLANES, NB):
+            for j in range(s_planes(u), NB):
                 k = col(c, h, j)
                 nc.vector.tensor_scalar_mul(
                     out=up[:, j, :], in0=chunk[c]["xt"][:, j, h * HD : (h + 1) * HD], scalar1=dt_col[:, k : k + 1]
@@ -217,12 +227,12 @@ def tile_model_t_kernel(tc, cb, x, dt, dA_cumsum, C, prev_states, D, out):
             c, h = divmod(u, NH)
             wg3 = wgs[u % 2][:].rearrange("p (l j) -> p l j", j=NB)
             dec = unit[u]["dec"]
-            for i in range(NB):
+            for l0, nl, nj, view in chunk[c]["cbT"]:
                 nc.vector.scalar_tensor_tensor(
-                    out=wg3[:, i * P : (i + 1) * P, 0 : i + 1],
-                    in0=dec[:, 0 : i + 1, i * P : (i + 1) * P].rearrange("p j l -> p l j"),
+                    out=wg3[:, l0 : l0 + nl, 0:nj],
+                    in0=dec[:, 0:nj, l0 : l0 + nl].rearrange("p j l -> p l j"),
                     scalar=BIG,
-                    in1=chunk[c]["cbT"][i].rearrange("p j l -> p l j"),
+                    in1=view.rearrange("p j l -> p l j"),
                     op0=ALU.min,
                     op1=ALU.mult,
                 )

@@ -50,7 +50,7 @@ def tile_model_t_kernel(tc, cb, x, dt, dA_cumsum, C, prev_states, D, out):
             return h * (NCH * NB) + c * NB + i
 
         def s_planes(u):
-            return u % 2
+            return 2
 
         def ndirect(u):
             return NB if u == UNITS - 1 else NDIRECT

@@ -50,7 +50,7 @@ def tile_model_t_kernel(tc, cb, x, dt, dA_cumsum, C, prev_states, D, out):
             return h * (NCH * NB) + c * NB + i
 
         def s_planes(u):
-            return 2
+            return 1
 
         def ndirect(u):
             return NB if u == UNITS - 1 else NDIRECT
@@ -96,8 +96,8 @@ def tile_model_t_kernel(tc, cb, x, dt, dA_cumsum, C, prev_states, D, out):
 
         wgs = []
         for k in range(2):
-            wg = const.tile([P, L * NB], BF16, name="wg%d" % k, align_bytes=64)
-            nc.vector.memset(wg[:], 0.0)
+            wg = const.tile([P, (2 - k) * L * NB], BF16, name="wg%d" % k, align_bytes=64)
+            nc.vector.memset(wg[:, 0 : L * NB], 0.0)
             wgs.append(wg)
 
         decs = []
@@ -225,7 +225,7 @@ def tile_model_t_kernel(tc, cb, x, dt, dA_cumsum, C, prev_states, D, out):
 
         def stage_w(u):
             c, h = divmod(u, NH)
-            wg3 = wgs[u % 2][:].rearrange("p (l j) -> p l j", j=NB)
+            wg3 = wgs[u % 2][:, 0 : L * NB].rearrange("p (l j) -> p l j", j=NB)
             dec = unit[u]["dec"]
             for l0, nl, nj, view in chunk[c]["cbT"]:
                 nc.vector.scalar_tensor_tensor(
@@ -238,28 +238,28 @@ def tile_model_t_kernel(tc, cb, x, dt, dA_cumsum, C, prev_states, D, out):
                 )
 
         def regroup_u(u, copier):
-            ug = work.tile([P, HD, NB], BF16, name="ug", tag="ug", bufs=3, align_bytes=64)
+            lo = L * NB + (u % 2) * HD * NB
             copier(
-                out=ug[:].rearrange("p (c i) t -> p c t i", i=4),
+                out=wgs[0][:, lo : lo + HD * NB].rearrange("p (c i t) -> p c t i", i=4, t=NB),
                 in_=unit[u]["up"][:].rearrange("p t (c i) -> p c t i", i=4),
             )
-            unit[u]["ug"] = ug
 
-        def quant_w(u):
-            wq = work.tile([P, L], U32, name="wq", tag="wq", bufs=2, align_bytes=64)
-            ws = work.tile([P, L], U8, name="ws", tag="ws", bufs=2, align_bytes=64)
-            nc.vector.quantize_mx(out=wq[:].bitcast(FP8X4), scales=ws[:], in_=wgs[u % 2][:])
-            unit[u]["wq"] = wq
-            unit[u]["ws"] = ws
-
-        def quant_u(u):
-            uq = work.tile([P, HD], U32, name="uq", tag="uq", bufs=2, align_bytes=64)
-            us = work.tile([P, HD], U8, name="us", tag="us", bufs=2, align_bytes=64)
-            nc.vector.quantize_mx(
-                out=uq[:].bitcast(FP8X4), scales=us[:], in_=unit[u]["ug"][:].rearrange("p c t -> p (c t)")
-            )
-            unit[u]["uq"] = uq
-            unit[u]["us"] = us
+        def quant(u):
+            if u % 2 == 0:
+                qa = work.tile([P, L + 2 * HD], U32, name="qa", tag="qa", bufs=2, align_bytes=64)
+                sa = work.tile([P, L + 2 * HD], U8, name="sa", tag="sa", bufs=2, align_bytes=64)
+                nc.vector.quantize_mx(out=qa[:].bitcast(FP8X4), scales=sa[:], in_=wgs[0][:])
+                unit[u]["wq"] = qa[:, 0:L]
+                unit[u]["ws"] = sa[:, 0:L]
+                for v in range(2):
+                    unit[u + v]["uq"] = qa[:, L + v * HD : L + (v + 1) * HD]
+                    unit[u + v]["us"] = sa[:, L + v * HD : L + (v + 1) * HD]
+            else:
+                qb = work.tile([P, L], U32, name="qb", tag="qb", bufs=2, align_bytes=64)
+                sb = work.tile([P, L], U8, name="sb", tag="sb", bufs=2, align_bytes=64)
+                nc.vector.quantize_mx(out=qb[:].bitcast(FP8X4), scales=sb[:], in_=wgs[1][:])
+                unit[u]["wq"] = qb[:, 0:L]
+                unit[u]["ws"] = sb[:, 0:L]
 
         def stage_m(u):
             ys = []
@@ -271,8 +271,8 @@ def tile_model_t_kernel(tc, cb, x, dt, dA_cumsum, C, prev_states, D, out):
                         out=y[:, b, :],
                         lhsT=unit[u]["wq"][:, i * P : (i + 1) * P].bitcast(FP8X4),
                         lhsT_scale=unit[u]["ws"][:, i * P : (i + 1) * P],
-                        rhs=unit[u]["uq"][:].bitcast(FP8X4),
-                        rhs_scale=unit[u]["us"][:],
+                        rhs=unit[u]["uq"].bitcast(FP8X4),
+                        rhs_scale=unit[u]["us"],
                         start=True,
                         stop=True,
                     )
@@ -344,7 +344,6 @@ def tile_model_t_kernel(tc, cb, x, dt, dA_cumsum, C, prev_states, D, out):
                     mask_chunk(c + 1)
                 if k + 2 < UNITS:
                     planes_v(k + 2)
-                quant_u(k)
-                quant_w(k)
+                quant(k)
                 if h == 1 and c + 2 < NCH:
                     load_chunk(c + 2)

from contextlib import ExitStack

import concourse.mybir as mybir
from concourse.masks import make_identity

FLOPS = 2 * 32 * 512 * 512 * 256 + 2 * 32 * 512 * 256 * 128

BF16 = mybir.dt.bfloat16
F32 = mybir.dt.float32
U32 = mybir.dt.uint32
U8 = mybir.dt.uint8
FP8X4 = mybir.dt.float8_e4m3fn_x4
ACT = mybir.ActivationFunctionType
ALU = mybir.AluOpType

P = 128
NCH = 8
NH = 4
L = 512
NB = 4
HD = 256
UNITS = NCH * NH
BIG = 3.0e38
NDIRECT = 0
CB_PITCH = 640


def tile_model_t_kernel(tc, cb, x, dt, dA_cumsum, C, prev_states, D, out):
    nc = tc.nc

    cb_v = cb.rearrange("b c g (i m) s -> (b c g) m i s", m=P)
    x_v = x.rearrange("b (c j p) h d -> (b c) p j (h d)", j=NB, p=P)
    out_v = out.rearrange("b (c i p) h d -> (b c) p i (h d)", i=NB, p=P)
    c_v = C.rearrange("b (c i m) g n -> (b c) m i (g n)", i=NB, m=P)
    pv_v = prev_states.rearrange("b c h (q m) n -> (b c) m (h q) n", m=P)
    da_rows_v = dA_cumsum.rearrange("b h c (i m) -> (b h c i) m", m=P)
    dt_rows_v = dt.rearrange("b h c (i m) -> (b h c i) m", m=P)

    with ExitStack() as ctx:
        const = ctx.enter_context(tc.tile_pool(name="const", bufs=1))
        loads = ctx.enter_context(tc.tile_pool(name="loads", bufs=2))
        work = ctx.enter_context(tc.tile_pool(name="work", bufs=2))
        psum = ctx.enter_context(tc.psum_pool(name="psum", bufs=1))
        ctx.enter_context(tc.manual_schedule())

        chunk = {}
        unit = {}

        def col(c, h, i):
            return h * (NCH * NB) + c * NB + i

        def s_planes(u):
            return 1

        def ndirect(u):
            return NB if u == UNITS - 1 else NDIRECT

        def load_chunk(c):
            cbf = loads.tile([P, NB * (CB_PITCH + P)], BF16, name="cbf", tag="cbf", bufs=2)
            cbt = cbf[:, 0 : NB * CB_PITCH].rearrange("p (i w) -> p i w", w=CB_PITCH)[:, :, 0:L]
            nc.sync.dma_start(out=cbt, in_=cb_v[c])
            bc = loads.tile([P, NH, L], BF16, name="bc", tag="bc", bufs=3)
            nc.sync.dma_start(out=bc[:], in_=dA_cumsum[0, :, c, :].partition_broadcast(P))
            xt = loads.tile([P, NB, NH * HD], BF16, name="xt", tag="xt", bufs=3)
            nc.sync.dma_start(out=xt[:], in_=x_v[c])
            pv = loads.tile([P, 2 * NH, P], BF16, name="pv", tag="pv", bufs=2)
            nc.sync.dma_start(out=pv[:], in_=pv_v[c])
            cc = loads.tile([P, NB, P], BF16, name="cc", tag="cc", bufs=2)
            nc.sync.dma_start(out=cc[:], in_=c_v[c])
            chunk[c] = {"bc": bc, "cbf": cbf, "cbt": cbt, "xt": xt, "pv": pv, "cc": cc}

        da_rows = const.tile([P, P], BF16, name="da_rows")
        nc.scalar.dma_start(out=da_rows[:], in_=da_rows_v)
        dt_rows = const.tile([P, P], BF16, name="dt_rows")
        nc.scalar.dma_start(out=dt_rows[:], in_=dt_rows_v)
        d_bf = const.tile([P, NH], BF16, name="d_bf")
        nc.scalar.dma_start(out=d_bf[:], in_=D.partition_broadcast(P))
        load_chunk(0)
        load_chunk(1)

        ident = const.tile([P, P], BF16, name="ident")
        make_identity(nc, ident[:])
        maskf = const.tile([P, P], F32, name="maskf")
        nc.gpsimd.memset(maskf[:], 1.0)
        nc.gpsimd.affine_select(
            out=maskf[:],
            in_=maskf[:],
            compare_op=ALU.is_ge,
            fill=0.0,
            base=0,
            pattern=[[-1, P]],
            channel_multiplier=1,
        )
        maskb = const.tile([P, P], BF16, name="maskb")
        nc.vector.tensor_copy(out=maskb[:], in_=maskf[:])

        wgs = []
        for k in range(2):
            wg = const.tile([P, (2 - k) * L * NB], BF16, name="wg%d" % k, align_bytes=64)
            nc.vector.memset(wg[:, 0 : L * NB], 0.0)
            wgs.append(wg)

        decs = []
        for k in range(3):
            dec_k = const.tile([P, NB, L], F32, name="dec%d" % k)
            nc.vector.memset(dec_k[:, 1, 0:P], 0.0)
            decs.append(dec_k)
        zeros = const.tile([P, P], BF16, name="zeros")
        nc.vector.memset(zeros[:], 0.0)

        d_col = const.tile([P, NH], F32, name="d_col")
        nc.vector.tensor_copy(out=d_col[:], in_=d_bf[:])

        da_t = psum.tile([P, P], BF16, name="da_t", tag="tp", bufs=2)
        nc.tensor.transpose(out=da_t[:], in_=da_rows[:], identity=ident[:])
        e_a = const.tile([P, P], F32, name="e_a")
        nc.scalar.activation(out=e_a[:], in_=da_t[:], func=ACT.Exp)
        neg_da = const.tile([P, P], F32, name="neg_da")
        nc.scalar.activation(out=neg_da[:], in_=da_t[:], func=ACT.Copy, scale=-1.0)
        dt_t = psum.tile([P, P], BF16, name="dt_t", tag="tp", bufs=2)
        nc.tensor.transpose(out=dt_t[:], in_=dt_rows[:], identity=ident[:])
        dt_col = const.tile([P, P], F32, name="dt_col")
        nc.scalar.copy(out=dt_col[:], in_=dt_t[:])

        def mask_chunk(c):
            diag = chunk[c]["cbf"][:].rearrange("p (i w) -> p i w", w=CB_PITCH + P)[:, :, 0:P]
            nc.vector.tensor_tensor(
                out=diag, in0=diag, in1=maskb[:].unsqueeze(1).to_broadcast([P, NB, P]), op=ALU.mult
            )

        def prep_pe(c):
            cc_t = psum.tile([P, NB, P], BF16, name="cc_t", tag="tp", bufs=2)
            for i in range(NB):
                nc.tensor.transpose(out=cc_t[:, i, :], in_=chunk[c]["cc"][:, i, :], identity=ident[:])
            pv_t = psum.tile([P, 2 * NH, P], BF16, name="pv_t", tag="tp", bufs=2)
            for q in range(2 * NH):
                nc.tensor.transpose(out=pv_t[:, q, :], in_=chunk[c]["pv"][:, q, :], identity=ident[:])
            chunk[c]["cc_t"] = cc_t
            chunk[c]["pv_t"] = pv_t

        def prep_copy(c):
            ct = work.tile([P, NB, P], BF16, name="ct", tag="ct", bufs=2)
            nc.scalar.copy(out=ct[:], in_=chunk[c]["cc_t"][:])
            pt = work.tile([P, 2 * NH, P], BF16, name="pt", tag="pt", bufs=2)
            nc.scalar.copy(out=pt[:], in_=chunk[c]["pv_t"][:])
            chunk[c]["ct"] = ct
            chunk[c]["pt"] = pt

        def cbt_chunk(c):
            cbt = chunk[c]["cbt"]
            ta = psum.tile([P, 7 * P], BF16, name="cbta", tag="cbta", bufs=1)
            tb = psum.tile([P, 4 * P], BF16, name="cbtb", tag="cbtb", bufs=1)
            v01 = ta[:, 0 : 4 * P].rearrange("p (j l) -> p j l", j=2)
            v2 = ta[:, 4 * P : 7 * P].rearrange("p (j l) -> p j l", j=3)
            v3 = tb[:].rearrange("p (j l) -> p j l", j=4)
            nc.tensor.transpose(out=v01[:, 0, 0:P], in_=cbt[:, 0, 0:P], identity=ident[:])
            nc.tensor.transpose(out=v01[:, 1, 0:P], in_=zeros[:], identity=ident[:])
            for j in range(2):
                nc.tensor.transpose(out=v01[:, j, P : 2 * P], in_=cbt[:, 1, j * P : (j + 1) * P], identity=ident[:])
            for j in range(3):
                nc.tensor.transpose(out=v2[:, j, :], in_=cbt[:, 2, j * P : (j + 1) * P], identity=ident[:])
            for j in range(4):
                nc.tensor.transpose(out=v3[:, j, :], in_=cbt[:, 3, j * P : (j + 1) * P], identity=ident[:])
            chunk[c]["cbT"] = [(0, 2 * P, 2, v01), (2 * P, P, 3, v2), (3 * P, P, 4, v3)]

        def stage_s(u):
            c, h = divmod(u, NH)
            dec = decs[u % 3]
            for j in range(NB):
                k = col(c, h, j)
                nc.scalar.activation(
                    out=dec[:, j, j * P :],
                    in_=chunk[c]["bc"][:, h, j * P :],
                    func=ACT.Exp,
                    bias=neg_da[:, k : k + 1],
                    scale=1.0,
                )
            for j in range(s_planes(u)):
                k = col(c, h, j)
                nc.scalar.activation(
                    out=unit[u]["up"][:, j, :],
                    in_=chunk[c]["xt"][:, j, h * HD : (h + 1) * HD],
                    func=ACT.Copy,
                    scale=dt_col[:, k : k + 1],
                )
            unit[u]["dec"] = dec
            regroup_u(u, nc.scalar.copy)

        def planes_v(u):
            c, h = divmod(u, NH)
            up = work.tile([P, NB, HD], BF16, name="up", tag="up", bufs=3)
            for j in range(s_planes(u), NB):
                k = col(c, h, j)
                nc.vector.tensor_scalar_mul(
                    out=up[:, j, :], in0=chunk[c]["xt"][:, j, h * HD : (h + 1) * HD], scalar1=dt_col[:, k : k + 1]
                )
            unit[u] = {"up": up}

        def stage_z(u):
            c, h = divmod(u, NH)
            nd = ndirect(u)
            tz = None
            if nd < NB:
                tz = work.tile([P, NB - nd, HD], F32, name="tz", tag="tz", bufs=4)
            zs = []
            for a in range(2):
                z = psum.tile([P, 2, HD], F32, name="z", tag="z", bufs=2)
                for b in range(2):
                    i = 2 * a + b
                    nc.tensor.matmul(
                        out=z[:, b, :],
                        lhsT=chunk[c]["ct"][:, i, :],
                        rhs=chunk[c]["pt"][:, 2 * h : 2 * h + 2, :].rearrange("p q m -> p (q m)"),
                        start=True,
                        stop=True,
                    )
                for b in range(2):
                    i = 2 * a + b
                    k = col(c, h, i)
                    if i < NB - nd:
                        nc.scalar.activation(out=tz[:, i, :], in_=z[:, b, :], func=ACT.Copy, scale=e_a[:, k : k + 1])
                zs.append(z)
            unit[u]["tz"] = tz
            unit[u]["z"] = zs

        def stage_w(u):
            c, h = divmod(u, NH)
            wg3 = wgs[u % 2][:, 0 : L * NB].rearrange("p (l j) -> p l j", j=NB)
            dec = unit[u]["dec"]
            for l0, nl, nj, view in chunk[c]["cbT"]:
                nc.vector.scalar_tensor_tensor(
                    out=wg3[:, l0 : l0 + nl, 0:nj],
                    in0=dec[:, 0:nj, l0 : l0 + nl].rearrange("p j l -> p l j"),
                    scalar=BIG,
                    in1=view.rearrange("p j l -> p l j"),
                    op0=ALU.min,
                    op1=ALU.mult,
                )

        def regroup_u(u, copier):
            lo = L * NB + (u % 2) * HD * NB
            copier(
                out=wgs[0][:, lo : lo + HD * NB].rearrange("p (c i t) -> p c t i", i=4, t=NB),
                in_=unit[u]["up"][:].rearrange("p t (c i) -> p c t i", i=4),
            )

        def quant(u):
            if u % 2 == 0:
                qa = work.tile([P, L + 2 * HD], U32, name="qa", tag="qa", bufs=2, align_bytes=64)
                sa = work.tile([P, L + 2 * HD], U8, name="sa", tag="sa", bufs=2, align_bytes=64)
                nc.vector.quantize_mx(out=qa[:].bitcast(FP8X4), scales=sa[:], in_=wgs[0][:])
                unit[u]["wq"] = qa[:, 0:L]
                unit[u]["ws"] = sa[:, 0:L]
                for v in range(2):
                    unit[u + v]["uq"] = qa[:, L + v * HD : L + (v + 1) * HD]
                    unit[u + v]["us"] = sa[:, L + v * HD : L + (v + 1) * HD]
            else:
                qb = work.tile([P, L], U32, name="qb", tag="qb", bufs=2, align_bytes=64)
                sb = work.tile([P, L], U8, name="sb", tag="sb", bufs=2, align_bytes=64)
                nc.vector.quantize_mx(out=qb[:].bitcast(FP8X4), scales=sb[:], in_=wgs[1][:])
                unit[u]["wq"] = qb[:, 0:L]
                unit[u]["ws"] = sb[:, 0:L]

        def stage_m(u):
            ys = []
            for a in range(2):
                y = psum.tile([P, 2, HD], F32, name="y", tag="y", bufs=2)
                for b in range(2):
                    i = 2 * a + b
                    nc.tensor.matmul_mx(
                        out=y[:, b, :],
                        lhsT=unit[u]["wq"][:, i * P : (i + 1) * P].bitcast(FP8X4),
                        lhsT_scale=unit[u]["ws"][:, i * P : (i + 1) * P],
                        rhs=unit[u]["uq"].bitcast(FP8X4),
                        rhs_scale=unit[u]["us"],
                        start=True,
                        stop=True,
                    )
                ys.append(y)
            unit[u]["y"] = ys

        def stage_e(u):
            c, h = divmod(u, NH)
            o = work.tile([P, NB, HD], F32, name="o", tag="o", bufs=3)
            tz = unit[u]["tz"]
            nd = ndirect(u)
            for a in (1, 0):
                nc.vector.scalar_tensor_tensor(
                    out=o[:, 2 * a : 2 * a + 2, :],
                    in0=chunk[c]["xt"][:, 2 * a : 2 * a + 2, h * HD : (h + 1) * HD],
                    scalar=d_col[:, h : h + 1],
                    in1=unit[u]["y"][a][:],
                    op0=ALU.mult,
                    op1=ALU.add,
                )
                lo = 2 * a
                hi = min(2 * a + 2, NB - nd)
                if hi > lo:
                    nc.gpsimd.tensor_tensor(out=o[:, lo:hi, :], in0=o[:, lo:hi, :], in1=tz[:, lo:hi, :], op=ALU.add)
            for i in reversed(range(NB - nd, NB)):
                k = col(c, h, i)
                nc.vector.scalar_tensor_tensor(
                    out=o[:, i, :],
                    in0=unit[u]["z"][i // 2][:, i % 2, :],
                    scalar=e_a[:, k : k + 1],
                    in1=o[:, i, :],
                    op0=ALU.mult,
                    op1=ALU.add,
                )
                if nd == NB and i == 2:
                    nc.sync.dma_start(out=out_v[c][:, 2:NB, h * HD : (h + 1) * HD], in_=o[:, 2:NB, :])
            if nd == NB:
                nc.sync.dma_start(out=out_v[c][:, 0:2, h * HD : (h + 1) * HD], in_=o[:, 0:2, :])
            else:
                nc.sync.dma_start(out=out_v[c][:, :, h * HD : (h + 1) * HD], in_=o[:])

        mask_chunk(0)
        cbt_chunk(0)
        planes_v(0)
        planes_v(1)
        stage_s(0)
        for k in range(UNITS + 2):
            c, h = divmod(k, NH)
            if k + 1 < UNITS:
                stage_s(k + 1)
            if k == 0:
                prep_pe(0)
                prep_copy(0)
            if k < UNITS:
                stage_z(k)
            if k >= 2:
                stage_e(k - 2)
            if 1 <= k <= UNITS:
                stage_m(k - 1)
            if k < UNITS:
                if h == 2 and c + 1 < NCH:
                    prep_pe(c + 1)
                stage_w(k)
                if h == 2 and c + 1 < NCH:
                    prep_copy(c + 1)
                if h == 3 and c + 1 < NCH:
                    cbt_chunk(c + 1)
                if h == 1 and c + 1 < NCH:
                    mask_chunk(c + 1)
                if k + 2 < UNITS:
                    planes_v(k + 2)
                quant(k)
                if h == 1 and c + 2 < NCH:
                    load_chunk(c + 2)
